import numpy as np
import ml_dtypes


def mxq(x, axis, fmt="e4m3"):
    dtype, down = {"e4m3": (ml_dtypes.float8_e4m3fn, 7), "e5m2": (ml_dtypes.float8_e5m2, 14)}[fmt]
    v = np.moveaxis(np.asarray(x, np.float32).astype(ml_dtypes.bfloat16).astype(np.float64), axis, -1)
    blocks = v.reshape(v.shape[:-1] + (-1, 32))
    amax = np.abs(blocks).max(-1, keepdims=True)
    byte = np.maximum(np.where(amax > 0, np.frexp(amax)[1] - 1 + 127, 0) - down, 1)
    scale = np.exp2(byte - 127.0)
    codes = (blocks / scale).astype(np.float32).astype(dtype).astype(np.float64)
    return np.moveaxis((codes * scale).reshape(v.shape), -1, axis)


WIDE = False


def mx_kscale(k):
    if not WIDE:
        return np.ones(k)
    levels = np.array([10, -10, 5, -5, 0])
    a = np.random.permutation(np.resize(levels, k // 512 * 4)).reshape(k // 512, 4)
    idx = np.arange(k)
    return np.exp2(a[idx // 512, idx % 128 // 32])


BF16 = ml_dtypes.bfloat16


def bf(x):
    return np.asarray(x, np.float32).astype(BF16)


def f64(x):
    return np.asarray(x).astype(np.float64)


B, K, N, F = 8, 4, 512, 128


def sigmoid(v):
    return 1.0 / (1.0 + np.exp(-v))


def setup_inputs():
    t = mx_kscale(K * F)[:F]
    return {"H": bf(np.random.standard_normal((B, N, F)) * t),
            "E": bf(np.random.random((B, K, N, N)) * 10.0 / N),
            "RW": bf(np.random.standard_normal((F, F, K)) * 0.7 * np.sqrt(K * N / F) / t[:, None, None]),
            "SW": bf(np.random.standard_normal((F, F)) / np.sqrt(F) / t[:, None])}


def reference(H, E, RW, SW):
    Hf, Ef = f64(H), f64(E)
    n = Ef.shape[2]
    D = 1.0 / (Ef + np.eye(n)).sum(axis=(1, 2))
    G = mxq(Ef, 3, "e4m3") @ mxq(Hf, 1, "e4m3")[:, None]
    X = G.transpose(0, 2, 1, 3).reshape(B, N, K * F)
    W = f64(RW).transpose(2, 0, 1).reshape(K * F, F)
    rel = mxq(X, 2, "e4m3") @ mxq(W, 0, "e4m3")
    self_term = Hf @ f64(SW)
    return sigmoid(D[:, :, None] * rel + self_term)

@@ -1,0 +1,290 @@
+from contextlib import ExitStack
+
+import concourse.mybir as mybir
+from concourse.masks import make_identity
+
+F32 = mybir.dt.float32
+BF16 = mybir.dt.bfloat16
+U32 = mybir.dt.uint32
+U8 = mybir.dt.uint8
+FP8X4 = mybir.dt.float8_e4m3fn_x4
+ALU = mybir.AluOpType
+ACT = mybir.ActivationFunctionType
+
+P = 128
+NB = 8
+NK = 4
+NC = 4
+UNITS = NB * NC
+FLOPS = 2 * 8 * 4 * 512 * 512 * 128 + 2 * 8 * 512 * 512 * 128 + 2 * 8 * 512 * 128 * 128
+
+MANUAL = True
+EB = 12
+L1 = 3
+L2 = L1 + 1
+NCS = 8
+GS = 4
+
+
+def tile_rgcnconv_kernel(tc, H, E, RW, SW, out):
+    nc = tc.nc
+    with ExitStack() as ctx:
+        if MANUAL:
+            ctx.enter_context(tc.manual_schedule())
+        const = ctx.enter_context(tc.tile_pool(name="const", bufs=1))
+        epool = ctx.enter_context(tc.tile_pool(name="epool", bufs=EB))
+        grpp = ctx.enter_context(tc.tile_pool(name="grpp", bufs=3))
+        etp = ctx.enter_context(tc.tile_pool(name="etp", bufs=5))
+        g2p = ctx.enter_context(tc.tile_pool(name="g2p", bufs=3))
+        hwp = ctx.enter_context(tc.tile_pool(name="hwp", bufs=2))
+        htp = ctx.enter_context(tc.tile_pool(name="htp", bufs=3))
+        dpool = ctx.enter_context(tc.tile_pool(name="dpool", bufs=3))
+        tpool = ctx.enter_context(tc.tile_pool(name="tpool", bufs=3))
+        xtps = ctx.enter_context(tc.psum_pool(name="xtps", bufs=3))
+        gps = ctx.enter_context(tc.psum_pool(name="gps", bufs=2))
+        relps = ctx.enter_context(tc.psum_pool(name="relps", bufs=2))
+        csps = ctx.enter_context(tc.psum_pool(name="csps", bufs=1))
+
+        warm = const.tile([P, 1], F32, name="warm")
+        nc.vector.memset(warm[:], 0.0)
+        nc.scalar.activation(out=warm[:], in_=warm[:], func=ACT.Sigmoid)
+        ones = const.tile([P, NCS], BF16, name="ones")
+        nc.vector.memset(ones[:], 1.0)
+        ident32 = const.tile([P, P], F32, name="ident32")
+        make_identity(nc, ident32[:])
+        identbf = const.tile([P, P], BF16, name="identbf")
+        make_identity(nc, identbf[:])
+
+        sw_sb = const.tile([P, P], BF16, name="sw_sb")
+        nc.scalar.dma_start(out=sw_sb[:], in_=SW)
+        rw_sb = const.tile([P, 4 * P], BF16, name="rw_sb", align_bytes=64)
+        nc.scalar.dma_start(out=rw_sb[:], in_=RW.rearrange("m f k -> m (f k)"))
+
+        h_sb = const.tile([P, NB * 512], BF16, name="h_sb")
+        h_dst = h_sb[:].rearrange("q (g x) -> q g x", x=256)
+        h_src = H.rearrange("b (u q e) m -> (b u) q (e m)", u=2, q=P, e=2).rearrange("g q x -> q g x")
+        for ch in range(2):
+            nc.sync.dma_start(out=h_dst[:, 8 * ch : 8 * ch + 8, :], in_=h_src[:, 8 * ch : 8 * ch + 8, :])
+
+        e_tiles = {}
+
+        def load_e(n):
+            b, c = divmod(n, NC)
+            e_sb = epool.tile([P, NK * 512], BF16, name="e_sb")
+            nc.sync.dma_start(
+                out=e_sb[:].rearrange("p (k j) -> p k j", k=NK),
+                in_=E[b, :, P * c : P * c + P, :].rearrange("k p j -> p k j"),
+            )
+            e_tiles[n] = e_sb
+
+        for n in range(EB):
+            load_e(n)
+
+        wq = const.tile([P, P], U32, name="wq", align_bytes=64)
+        ws = const.tile([P, P], U8, name="ws", align_bytes=64)
+        nc.vector.quantize_mx(out=wq[:].bitcast(FP8X4), scales=ws[:], in_=rw_sb[:])
+
+        hq = const.tile([P, NB * P], U32, name="hq", align_bytes=64)
+        hs = const.tile([P, NB * P], U8, name="hs", align_bytes=64)
+        self_sb = const.tile([P, NB, 512], F32, name="self_sb")
+
+        def quantise_h(ch):
+            hgrp = hwp.tile([P, 2048], BF16, name="hgrp", align_bytes=64)
+            nc.vector.tensor_copy(
+                out=hgrp[:].rearrange("q (b m t) -> q b m t", b=4, m=P, t=4),
+                in_=h_sb[:, 2048 * ch : 2048 * ch + 2048].rearrange("q (b t m) -> q b m t", b=4, t=4, m=P),
+            )
+            return hgrp
+
+        def quantise_h2(ch, hgrp):
+            nc.vector.quantize_mx(
+                out=hq[:, 512 * ch : 512 * ch + 512].bitcast(FP8X4),
+                scales=hs[:, 512 * ch : 512 * ch + 512],
+                in_=hgrp[:],
+            )
+
+        ht_tiles = {}
+
+        def transpose_h(b):
+            hps = xtps.tile([P, 4, P], BF16, name="hps", tag="xt")
+            for t in range(4):
+                col = 512 * b + P * t
+                nc.tensor.transpose(hps[:, t, :], h_sb[:, col : col + P], identbf[:])
+            ht = htp.tile([P, 512], BF16, name="ht")
+            nc.scalar.copy(
+                out=ht[:].rearrange("m (u q e) -> m u q e", u=2, q=P, e=2),
+                in_=hps[:].rearrange("m (u e) q -> m u q e", u=2, e=2),
+            )
+            ht_tiles[b] = ht
+
+        def self_term(b):
+            sps = gps.tile([P, NC, P], F32, name="sps", tag="gb")
+            ht = ht_tiles[b]
+            for c in range(NC):
+                nc.tensor.matmul(
+                    out=sps[:, c, :], lhsT=ht[:, P * c : P * c + P], rhs=sw_sb[:], start=True, stop=True
+                )
+            src = sps[:].rearrange("p c f -> p (c f)")
+            if b % 4 == 3:
+                nc.scalar.copy(out=self_sb[:, b, :], in_=src)
+            else:
+                nc.vector.tensor_copy(out=self_sb[:, b, :], in_=src)
+
+        hg0 = quantise_h(0)
+        transpose_h(0)
+        quantise_h2(0, hg0)
+        for b in range(NB):
+            if b + 1 < NB:
+                transpose_h(b + 1)
+            self_term(b)
+        hg1 = quantise_h(1)
+
+        grp_tiles = {}
+        et_tiles = {}
+        gb_tiles = {}
+        g2_tiles = {}
+        gq_tiles = {}
+        rel_tiles = {}
+        cs_tiles = {}
+        d_tiles = {}
+        t_tiles = {}
+
+        def transposes(n):
+            e32 = e_tiles[n][:].bitcast(F32)
+            grp = grpp.tile([P, 2048], BF16, name="grp", align_bytes=64)
+            grp32 = grp[:].bitcast(F32)
+            for h in range(2):
+                xt = xtps.tile([P, 4, P], F32, name="xt", tag="xt")
+                for s in range(4):
+                    col = 512 * h + P * s
+                    nc.tensor.transpose(xt[:, s, :], e32[:, col : col + P], ident32[:])
+                nc.scalar.copy(
+                    out=grp32[:, 512 * h : 512 * h + 512].rearrange("q (k p u) -> q k p u", k=2, p=P, u=2),
+                    in_=xt[:].rearrange("q (k u) p -> q k p u", k=2, u=2),
+                )
+            grp_tiles[n] = grp
+
+        def colsums(n):
+            b, c = divmod(n, NC)
+            if c == 0:
+                cs_new = csps.tile([P, NC, NC, NCS], F32, name="cs")
+                cs_tiles[b] = cs_new
+            cs = cs_tiles[b]
+            e_sb = e_tiles[n]
+            for cj in range(NC):
+                for k in range(NK):
+                    col = 512 * k + P * cj
+                    nc.tensor.matmul(
+                        out=cs[:, cj, c, :],
+                        lhsT=e_sb[:, col : col + P],
+                        rhs=ones[:],
+                        start=(k == 0),
+                        stop=(k == NK - 1),
+                    )
+
+        def quantise_e(n):
+            etq = etp.tile([P, 512], U32, name="etq", align_bytes=64)
+            ets = etp.tile([P, 512], U8, name="ets", align_bytes=64)
+            nc.vector.quantize_mx(out=etq[:].bitcast(FP8X4), scales=ets[:], in_=grp_tiles[n][:])
+            et_tiles[n] = (etq, ets)
+
+        def stage1(g):
+            b, c = divmod(g, NC)
+            etq, ets = et_tiles[g]
+            gb = gps.tile([P, NK, P], F32, name="gb", tag="gb")
+            for k in range(NK):
+                nc.tensor.matmul_mx(
+                    out=gb[:, k, :],
+                    lhsT=hq[:, P * b : P * b + P].bitcast(FP8X4),
+                    lhsT_scale=hs[:, P * b : P * b + P],
+                    rhs=etq[:, P * k : P * k + P].bitcast(FP8X4),
+                    rhs_scale=ets[:, P * k : P * k + P],
+                    start=True,
+                    stop=True,
+                )
+            g2 = g2p.tile([P, P, NK], BF16, name="g2", align_bytes=64)
+            src = gb[:].rearrange("m k i -> m i k")
+            if g % GS == GS - 1:
+                nc.scalar.copy(out=g2[:], in_=src)
+            else:
+                nc.vector.tensor_copy(out=g2[:], in_=src)
+            g2_tiles[g] = g2
+
+        def quantise_g(g):
+            gq = g2p.tile([P, P], U32, name="gq", align_bytes=64)
+            gs = g2p.tile([P, P], U8, name="gs", align_bytes=64)
+            nc.vector.quantize_mx(
+                out=gq[:].bitcast(FP8X4), scales=gs[:], in_=g2_tiles[g][:].rearrange("m i k -> m (i k)")
+            )
+            gq_tiles[g] = (gq, gs)
+
+        def stage2(g):
+            b, c = divmod(g, NC)
+            if c == 0:
+                rel_new = relps.tile([P, NC, P], F32, name="rel")
+                rel_tiles[b] = rel_new
+            gq, gs = gq_tiles[g]
+            nc.tensor.matmul_mx(
+                out=rel_tiles[b][:, c, :],
+                lhsT=gq[:].bitcast(FP8X4),
+                lhsT_scale=gs[:],
+                rhs=wq[:].bitcast(FP8X4),
+                rhs_scale=ws[:],
+                start=True,
+                stop=True,
+            )
+
+        def combine(g):
+            b, c = divmod(g, NC)
+            if c == 0:
+                t_new = tpool.tile([P, NC, P], F32, name="t")
+                t_tiles[b] = t_new
+            nc.vector.scalar_tensor_tensor(
+                out=t_tiles[b][:, c, :],
+                in0=rel_tiles[b][:, c, :],
+                scalar=d_tiles[b][:, c : c + 1],
+                in1=self_sb[:, b, P * c : P * c + P],
+                op0=ALU.mult,
+                op1=ALU.add,
+            )
+
+        def degrees(b):
+            ssum = dpool.tile([P, NC], F32, name="ssum")
+            nc.vector.tensor_reduce(
+                out=ssum[:], in_=cs_tiles[b][:, :, :, 0], axis=mybir.AxisListType.X, op=ALU.add
+            )
+            nc.vector.tensor_scalar_add(out=ssum[:], in0=ssum[:], scalar1=4.0)
+            d = dpool.tile([P, NC], F32, name="d")
+            nc.vector.reciprocal(out=d[:], in_=ssum[:])
+            d_tiles[b] = d
+
+        def finish(b):
+            t = t_tiles[b]
+            nc.scalar.activation(out=t[:], in_=t[:], func=ACT.Sigmoid)
+            nc.scalar.dma_start(out=out[b].rearrange("(c p) f -> p c f", p=P), in_=t[:])
+
+        for n in range(UNITS + L2 + 2):
+            g1 = n - L1
+            g2i = n - L2
+            if 0 <= g1 < UNITS:
+                stage1(g1)
+            if 0 <= g2i < UNITS:
+                stage2(g2i)
+            if n < UNITS:
+                transposes(n)
+                colsums(n)
+                if n + EB < UNITS:
+                    load_e(n + EB)
+            if n == 1:
+                quantise_h2(1, hg1)
+            if 0 <= n - 1 < UNITS:
+                quantise_e(n - 1)
+            if 0 <= g1 < UNITS:
+                quantise_g(g1)
+            if 0 <= g2i < UNITS:
+                combine(g2i)
+            if n < UNITS and n % NC == NC - 1:
+                degrees(n // NC)
+            gf = n - L2 - 1
+            if 0 <= gf < UNITS and gf % NC == NC - 1:
+                finish(gf // NC)

@@ -20,10 +20,18 @@ FLOPS = 2 * 8 * 4 * 512 * 512 * 128 + 2 * 8 * 512 * 512 * 128 + 2 * 8 * 512 * 12
 
 MANUAL = True
 EB = 12
-L1 = 3
-L2 = L1 + 1
 NCS = 8
-GS = 4
+REP = 1
+LAG_M1 = 2
+LAG_M2 = 4
+LAG_GC = 3
+LAG_QE = 1
+LAG_QG = 3
+LAG_ST = 5
+LAG_FIN = 6
+DEFER = 4
+HOFF = 1
+H_AFTER = {1: 0, 2: 1, 3: 2, 4: 3}
 
 
 def tile_rgcnconv_kernel(tc, H, E, RW, SW, out):
@@ -34,7 +42,7 @@ def tile_rgcnconv_kernel(tc, H, E, RW, SW, out):
         const = ctx.enter_context(tc.tile_pool(name="const", bufs=1))
         epool = ctx.enter_context(tc.tile_pool(name="epool", bufs=EB))
         grpp = ctx.enter_context(tc.tile_pool(name="grpp", bufs=3))
-        etp = ctx.enter_context(tc.tile_pool(name="etp", bufs=5))
+        etp = ctx.enter_context(tc.tile_pool(name="etp", bufs=4))
         g2p = ctx.enter_context(tc.tile_pool(name="g2p", bufs=3))
         hwp = ctx.enter_context(tc.tile_pool(name="hwp", bufs=2))
         htp = ctx.enter_context(tc.tile_pool(name="htp", bufs=3))
@@ -63,8 +71,9 @@ def tile_rgcnconv_kernel(tc, H, E, RW, SW, out):
         h_sb = const.tile([P, NB * 512], BF16, name="h_sb")
         h_dst = h_sb[:].rearrange("q (g x) -> q g x", x=256)
         h_src = H.rearrange("b (u q e) m -> (b u) q (e m)", u=2, q=P, e=2).rearrange("g q x -> q g x")
-        for ch in range(2):
-            nc.sync.dma_start(out=h_dst[:, 8 * ch : 8 * ch + 8, :], in_=h_src[:, 8 * ch : 8 * ch + 8, :])
+
+        def load_h(j):
+            nc.sync.dma_start(out=h_dst[:, 4 * j : 4 * j + 4, :], in_=h_src[:, 4 * j : 4 * j + 4, :])
 
         e_tiles = {}
 
@@ -79,6 +88,8 @@ def tile_rgcnconv_kernel(tc, H, E, RW, SW, out):
 
         for n in range(EB):
             load_e(n)
+            if n in H_AFTER:
+                load_h(H_AFTER[n])
 
         wq = const.tile([P, P], U32, name="wq", align_bytes=64)
         ws = const.tile([P, P], U8, name="ws", align_bytes=64)
@@ -88,18 +99,15 @@ def tile_rgcnconv_kernel(tc, H, E, RW, SW, out):
         hs = const.tile([P, NB * P], U8, name="hs", align_bytes=64)
         self_sb = const.tile([P, NB, 512], F32, name="self_sb")
 
-        def quantise_h(ch):
-            hgrp = hwp.tile([P, 2048], BF16, name="hgrp", align_bytes=64)
+        def quantise_h(j):
+            hgrp = hwp.tile([P, 1024], BF16, name="hgrp", align_bytes=64)
             nc.vector.tensor_copy(
-                out=hgrp[:].rearrange("q (b m t) -> q b m t", b=4, m=P, t=4),
-                in_=h_sb[:, 2048 * ch : 2048 * ch + 2048].rearrange("q (b t m) -> q b m t", b=4, t=4, m=P),
+                out=hgrp[:].rearrange("q (b m t) -> q b m t", b=2, m=P, t=4),
+                in_=h_sb[:, 1024 * j : 1024 * j + 1024].rearrange("q (b t m) -> q b m t", b=2, t=4, m=P),
             )
-            return hgrp
-
-        def quantise_h2(ch, hgrp):
             nc.vector.quantize_mx(
-                out=hq[:, 512 * ch : 512 * ch + 512].bitcast(FP8X4),
-                scales=hs[:, 512 * ch : 512 * ch + 512],
+                out=hq[:, 256 * j : 256 * j + 256].bitcast(FP8X4),
+                scales=hs[:, 256 * j : 256 * j + 256],
                 in_=hgrp[:],
             )
 
@@ -124,20 +132,7 @@ def tile_rgcnconv_kernel(tc, H, E, RW, SW, out):
                 nc.tensor.matmul(
                     out=sps[:, c, :], lhsT=ht[:, P * c : P * c + P], rhs=sw_sb[:], start=True, stop=True
                 )
-            src = sps[:].rearrange("p c f -> p (c f)")
-            if b % 4 == 3:
-                nc.scalar.copy(out=self_sb[:, b, :], in_=src)
-            else:
-                nc.vector.tensor_copy(out=self_sb[:, b, :], in_=src)
-
-        hg0 = quantise_h(0)
-        transpose_h(0)
-        quantise_h2(0, hg0)
-        for b in range(NB):
-            if b + 1 < NB:
-                transpose_h(b + 1)
-            self_term(b)
-        hg1 = quantise_h(1)
+            nc.scalar.copy(out=self_sb[:, b, :], in_=sps[:].rearrange("p c f -> p (c f)"))
 
         grp_tiles = {}
         et_tiles = {}
@@ -146,6 +141,7 @@ def tile_rgcnconv_kernel(tc, H, E, RW, SW, out):
         gq_tiles = {}
         rel_tiles = {}
         cs_tiles = {}
+        ss_tiles = {}
         d_tiles = {}
         t_tiles = {}
 
@@ -189,25 +185,24 @@ def tile_rgcnconv_kernel(tc, H, E, RW, SW, out):
             et_tiles[n] = (etq, ets)
 
         def stage1(g):
-            b, c = divmod(g, NC)
+            b = g // NC
             etq, ets = et_tiles[g]
             gb = gps.tile([P, NK, P], F32, name="gb", tag="gb")
-            for k in range(NK):
+            for rep in range(REP):
                 nc.tensor.matmul_mx(
-                    out=gb[:, k, :],
+                    out=gb[:].rearrange("m k i -> m (k i)"),
                     lhsT=hq[:, P * b : P * b + P].bitcast(FP8X4),
                     lhsT_scale=hs[:, P * b : P * b + P],
-                    rhs=etq[:, P * k : P * k + P].bitcast(FP8X4),
-                    rhs_scale=ets[:, P * k : P * k + P],
+                    rhs=etq[:].bitcast(FP8X4),
+                    rhs_scale=ets[:],
                     start=True,
                     stop=True,
                 )
+            gb_tiles[g] = gb
+
+        def copy_g(g):
             g2 = g2p.tile([P, P, NK], BF16, name="g2", align_bytes=64)
-            src = gb[:].rearrange("m k i -> m i k")
-            if g % GS == GS - 1:
-                nc.scalar.copy(out=g2[:], in_=src)
-            else:
-                nc.vector.tensor_copy(out=g2[:], in_=src)
+            nc.vector.tensor_copy(out=g2[:], in_=gb_tiles[g][:].rearrange("m k i -> m i k"))
             g2_tiles[g] = g2
 
         def quantise_g(g):
@@ -219,13 +214,10 @@ def tile_rgcnconv_kernel(tc, H, E, RW, SW, out):
             gq_tiles[g] = (gq, gs)
 
         def stage2(g):
-            b, c = divmod(g, NC)
-            if c == 0:
-                rel_new = relps.tile([P, NC, P], F32, name="rel")
-                rel_tiles[b] = rel_new
+            rel = relps.tile([P, P], F32, name="rel")
             gq, gs = gq_tiles[g]
             nc.tensor.matmul_mx(
-                out=rel_tiles[b][:, c, :],
+                out=rel[:],
                 lhsT=gq[:].bitcast(FP8X4),
                 lhsT_scale=gs[:],
                 rhs=wq[:].bitcast(FP8X4),
@@ -233,6 +225,7 @@ def tile_rgcnconv_kernel(tc, H, E, RW, SW, out):
                 start=True,
                 stop=True,
             )
+            rel_tiles[g] = rel
 
         def combine(g):
             b, c = divmod(g, NC)
@@ -241,50 +234,78 @@ def tile_rgcnconv_kernel(tc, H, E, RW, SW, out):
                 t_tiles[b] = t_new
             nc.vector.scalar_tensor_tensor(
                 out=t_tiles[b][:, c, :],
-                in0=rel_tiles[b][:, c, :],
+                in0=rel_tiles[g][:],
                 scalar=d_tiles[b][:, c : c + 1],
                 in1=self_sb[:, b, P * c : P * c + P],
                 op0=ALU.mult,
                 op1=ALU.add,
             )
 
-        def degrees(b):
+        def degree_sum(b):
             ssum = dpool.tile([P, NC], F32, name="ssum")
             nc.vector.tensor_reduce(
                 out=ssum[:], in_=cs_tiles[b][:, :, :, 0], axis=mybir.AxisListType.X, op=ALU.add
             )
+            ss_tiles[b] = ssum
+
+        def degree_inverse(b):
+            ssum = ss_tiles[b]
             nc.vector.tensor_scalar_add(out=ssum[:], in0=ssum[:], scalar1=4.0)
             d = dpool.tile([P, NC], F32, name="d")
             nc.vector.reciprocal(out=d[:], in_=ssum[:])
             d_tiles[b] = d
 
-        def finish(b):
+        def finish(b, c0, c1):
             t = t_tiles[b]
-            nc.scalar.activation(out=t[:], in_=t[:], func=ACT.Sigmoid)
-            nc.scalar.dma_start(out=out[b].rearrange("(c p) f -> p c f", p=P), in_=t[:])
+            nc.scalar.activation(out=t[:, c0:c1, :], in_=t[:, c0:c1, :], func=ACT.Sigmoid)
+            nc.scalar.dma_start(
+                out=out[b, P * c0 : P * c1, :].rearrange("(c p) f -> p c f", p=P), in_=t[:, c0:c1, :]
+            )
 
-        for n in range(UNITS + L2 + 2):
-            g1 = n - L1
-            g2i = n - L2
-            if 0 <= g1 < UNITS:
-                stage1(g1)
-            if 0 <= g2i < UNITS:
-                stage2(g2i)
+        def live(g):
+            return 0 <= g < UNITS
+
+        for n in range(UNITS + LAG_FIN + 1):
+            early_d = n % NC == 0 and NC <= n <= UNITS - DEFER
+            if early_d:
+                degree_sum(n // NC - 1)
             if n < UNITS:
                 transposes(n)
+            if n < UNITS - DEFER:
                 colsums(n)
-                if n + EB < UNITS:
-                    load_e(n + EB)
-            if n == 1:
-                quantise_h2(1, hg1)
-            if 0 <= n - 1 < UNITS:
-                quantise_e(n - 1)
-            if 0 <= g1 < UNITS:
-                quantise_g(g1)
-            if 0 <= g2i < UNITS:
-                combine(g2i)
-            if n < UNITS and n % NC == NC - 1:
-                degrees(n // NC)
-            gf = n - L2 - 1
-            if 0 <= gf < UNITS and gf % NC == NC - 1:
-                finish(gf // NC)
+            if UNITS <= n < UNITS + DEFER // 2:
+                colsums(UNITS - DEFER + 2 * (n - UNITS))
+                colsums(UNITS - DEFER + 2 * (n - UNITS) + 1)
+            if n + EB < UNITS:
+                load_e(n + EB)
+            m = n - HOFF
+            if 0 <= m < 2 * NB and m % 2 == 0:
+                transpose_h(m // 2)
+            if 0 <= m - 1 < 2 * NB and (m - 1) % 2 == 0:
+                self_term((m - 1) // 2)
+            if live(n - LAG_M1):
+                stage1(n - LAG_M1)
+            if live(n - LAG_M2):
+                stage2(n - LAG_M2)
+            if early_d:
+                degree_inverse(n // NC - 1)
+            if DEFER and n == UNITS + DEFER // 2 - 1:
+                degree_sum(NB - 1)
+                degree_inverse(NB - 1)
+            if live(n - LAG_GC):
+                copy_g(n - LAG_GC)
+            if live(n - LAG_QE):
+                quantise_e(n - LAG_QE)
+            if live(n - LAG_QG):
+                quantise_g(n - LAG_QG)
+            if live(n - LAG_ST):
+                combine(n - LAG_ST)
+            if 0 <= n - 1 < 4:
+                quantise_h(n - 1)
+            gf = n - LAG_FIN
+            if live(gf):
+                if gf < UNITS - NC:
+                    if gf % NC == NC - 1:
+                        finish(gf // NC, 0, NC)
+                else:
+                    finish(NB - 1, gf % NC, gf % NC + 1)

@@ -200,9 +200,16 @@ def tile_rgcnconv_kernel(tc, H, E, RW, SW, out):
                 )
             gb_tiles[g] = gb
 
+        def on_scalar(g):
+            return g % 4 == 1
+
         def copy_g(g):
             g2 = g2p.tile([P, P, NK], BF16, name="g2", align_bytes=64)
-            nc.vector.tensor_copy(out=g2[:], in_=gb_tiles[g][:].rearrange("m k i -> m i k"))
+            g_in = gb_tiles[g][:].rearrange("m k i -> m i k")
+            if on_scalar(g):
+                nc.scalar.copy(out=g2[:], in_=g_in)
+            else:
+                nc.vector.tensor_copy(out=g2[:], in_=g_in)
             g2_tiles[g] = g2
 
         def quantise_g(g):
@@ -269,6 +276,8 @@ def tile_rgcnconv_kernel(tc, H, E, RW, SW, out):
             early_d = n % NC == 0 and NC <= n <= UNITS - DEFER
             if early_d:
                 degree_sum(n // NC - 1)
+            if live(n - LAG_GC) and on_scalar(n - LAG_GC):
+                copy_g(n - LAG_GC)
             if n < UNITS:
                 transposes(n)
             if n < UNITS - DEFER:
@@ -292,7 +301,7 @@ def tile_rgcnconv_kernel(tc, H, E, RW, SW, out):
             if DEFER and n == UNITS + DEFER // 2 - 1:
                 degree_sum(NB - 1)
                 degree_inverse(NB - 1)
-            if live(n - LAG_GC):
+            if live(n - LAG_GC) and not on_scalar(n - LAG_GC):
                 copy_g(n - LAG_GC)
             if live(n - LAG_QE):
                 quantise_e(n - LAG_QE)

@@ -19,7 +19,7 @@ UNITS = NB * NC
 FLOPS = 2 * 8 * 4 * 512 * 512 * 128 + 2 * 8 * 512 * 512 * 128 + 2 * 8 * 512 * 128 * 128
 
 MANUAL = True
-EB = 12
+EB = 16
 NCS = 8
 REP = 1
 LAG_M1 = 2
@@ -29,9 +29,9 @@ LAG_QE = 1
 LAG_QG = 3
 LAG_ST = 5
 LAG_FIN = 6
-DEFER = 4
+LAG_CS = 2
 HOFF = 1
-H_AFTER = {1: 0, 2: 1, 3: 2, 4: 3}
+H_AFTER = {0: 0, 2: 1, 3: 2, 4: 3}
 
 
 def tile_rgcnconv_kernel(tc, H, E, RW, SW, out):
@@ -58,6 +58,8 @@ def tile_rgcnconv_kernel(tc, H, E, RW, SW, out):
         nc.scalar.activation(out=warm[:], in_=warm[:], func=ACT.Sigmoid)
         ones = const.tile([P, NCS], BF16, name="ones")
         nc.vector.memset(ones[:], 1.0)
+        fours = const.tile([P, NCS], BF16, name="fours")
+        nc.vector.memset(fours[:], 4.0)
         ident32 = const.tile([P, P], F32, name="ident32")
         make_identity(nc, ident32[:])
         identbf = const.tile([P, P], BF16, name="identbf")
@@ -80,10 +82,11 @@ def tile_rgcnconv_kernel(tc, H, E, RW, SW, out):
         def load_e(n):
             b, c = divmod(n, NC)
             e_sb = epool.tile([P, NK * 512], BF16, name="e_sb")
-            nc.sync.dma_start(
-                out=e_sb[:].rearrange("p (k j) -> p k j", k=NK),
-                in_=E[b, :, P * c : P * c + P, :].rearrange("k p j -> p k j"),
-            )
+            e_dst = e_sb[:].rearrange("p (k j) -> p k j", k=NK)
+            e_src = E[b, :, P * c : P * c + P, :].rearrange("k p j -> p k j")
+            step = 2 if n == 0 else NK
+            for k in range(0, NK, step):
+                nc.sync.dma_start(out=e_dst[:, k : k + step, :], in_=e_src[:, k : k + step, :])
             e_tiles[n] = e_sb
 
         for n in range(EB):
@@ -93,7 +96,6 @@ def tile_rgcnconv_kernel(tc, H, E, RW, SW, out):
 
         wq = const.tile([P, P], U32, name="wq", align_bytes=64)
         ws = const.tile([P, P], U8, name="ws", align_bytes=64)
-        nc.vector.quantize_mx(out=wq[:].bitcast(FP8X4), scales=ws[:], in_=rw_sb[:])
 
         hq = const.tile([P, NB * P], U32, name="hq", align_bytes=64)
         hs = const.tile([P, NB * P], U8, name="hs", align_bytes=64)
@@ -141,7 +143,6 @@ def tile_rgcnconv_kernel(tc, H, E, RW, SW, out):
         gq_tiles = {}
         rel_tiles = {}
         cs_tiles = {}
-        ss_tiles = {}
         d_tiles = {}
         t_tiles = {}
 
@@ -160,22 +161,21 @@ def tile_rgcnconv_kernel(tc, H, E, RW, SW, out):
                 )
             grp_tiles[n] = grp
 
-        def colsums(n):
-            b, c = divmod(n, NC)
-            if c == 0:
-                cs_new = csps.tile([P, NC, NC, NCS], F32, name="cs")
+        def colsums(b, cj):
+            if cj == 0:
+                cs_new = csps.tile([P, NC, NCS], F32, name="cs")
                 cs_tiles[b] = cs_new
             cs = cs_tiles[b]
-            e_sb = e_tiles[n]
-            for cj in range(NC):
+            nc.tensor.matmul(out=cs[:, cj, :], lhsT=identbf[:], rhs=fours[:], start=True, stop=False)
+            for c in range(NC):
                 for k in range(NK):
                     col = 512 * k + P * cj
                     nc.tensor.matmul(
-                        out=cs[:, cj, c, :],
-                        lhsT=e_sb[:, col : col + P],
+                        out=cs[:, cj, :],
+                        lhsT=e_tiles[NC * b + c][:, col : col + P],
                         rhs=ones[:],
-                        start=(k == 0),
-                        stop=(k == NK - 1),
+                        start=False,
+                        stop=(c == NC - 1 and k == NK - 1),
                     )
 
         def quantise_e(n):
@@ -201,7 +201,7 @@ def tile_rgcnconv_kernel(tc, H, E, RW, SW, out):
             gb_tiles[g] = gb
 
         def on_scalar(g):
-            return g % 4 == 1
+            return g % 8 == 1 or g >= UNITS - NC and g % 2 == 1
 
         def copy_g(g):
             g2 = g2p.tile([P, P, NK], BF16, name="g2", align_bytes=64)
@@ -248,24 +248,15 @@ def tile_rgcnconv_kernel(tc, H, E, RW, SW, out):
                 op1=ALU.add,
             )
 
-        def degree_sum(b):
-            ssum = dpool.tile([P, NC], F32, name="ssum")
-            nc.vector.tensor_reduce(
-                out=ssum[:], in_=cs_tiles[b][:, :, :, 0], axis=mybir.AxisListType.X, op=ALU.add
-            )
-            ss_tiles[b] = ssum
-
         def degree_inverse(b):
-            ssum = ss_tiles[b]
-            nc.vector.tensor_scalar_add(out=ssum[:], in0=ssum[:], scalar1=4.0)
             d = dpool.tile([P, NC], F32, name="d")
-            nc.vector.reciprocal(out=d[:], in_=ssum[:])
+            nc.vector.reciprocal(out=d[:], in_=cs_tiles[b][:, :, 0])
             d_tiles[b] = d
 
         def finish(b, c0, c1):
             t = t_tiles[b]
             nc.scalar.activation(out=t[:, c0:c1, :], in_=t[:, c0:c1, :], func=ACT.Sigmoid)
-            nc.scalar.dma_start(
+            nc.sync.dma_start(
                 out=out[b, P * c0 : P * c1, :].rearrange("(c p) f -> p c f", p=P), in_=t[:, c0:c1, :]
             )
 
@@ -273,18 +264,12 @@ def tile_rgcnconv_kernel(tc, H, E, RW, SW, out):
             return 0 <= g < UNITS
 
         for n in range(UNITS + LAG_FIN + 1):
-            early_d = n % NC == 0 and NC <= n <= UNITS - DEFER
-            if early_d:
-                degree_sum(n // NC - 1)
             if live(n - LAG_GC) and on_scalar(n - LAG_GC):
                 copy_g(n - LAG_GC)
             if n < UNITS:
                 transposes(n)
-            if n < UNITS - DEFER:
-                colsums(n)
-            if UNITS <= n < UNITS + DEFER // 2:
-                colsums(UNITS - DEFER + 2 * (n - UNITS))
-                colsums(UNITS - DEFER + 2 * (n - UNITS) + 1)
+            if live(n - LAG_CS):
+                colsums((n - LAG_CS) // NC, (n - LAG_CS) % NC)
             if n + EB < UNITS:
                 load_e(n + EB)
             m = n - HOFF
@@ -296,11 +281,6 @@ def tile_rgcnconv_kernel(tc, H, E, RW, SW, out):
                 stage1(n - LAG_M1)
             if live(n - LAG_M2):
                 stage2(n - LAG_M2)
-            if early_d:
-                degree_inverse(n // NC - 1)
-            if DEFER and n == UNITS + DEFER // 2 - 1:
-                degree_sum(NB - 1)
-                degree_inverse(NB - 1)
             if live(n - LAG_GC) and not on_scalar(n - LAG_GC):
                 copy_g(n - LAG_GC)
             if live(n - LAG_QE):
@@ -308,8 +288,14 @@ def tile_rgcnconv_kernel(tc, H, E, RW, SW, out):
             if live(n - LAG_QG):
                 quantise_g(n - LAG_QG)
             if live(n - LAG_ST):
+                if (n - LAG_ST) % NC == 0:
+                    degree_inverse((n - LAG_ST) // NC)
                 combine(n - LAG_ST)
-            if 0 <= n - 1 < 4:
+            if n == 0:
+                quantise_h(0)
+            if n == 1:
+                nc.vector.quantize_mx(out=wq[:].bitcast(FP8X4), scales=ws[:], in_=rw_sb[:])
+            if 2 <= n < 5:
                 quantise_h(n - 1)
             gf = n - LAG_FIN
             if live(gf):

@@ -18,10 +18,8 @@ NC = 4
 UNITS = NB * NC
 FLOPS = 2 * 8 * 4 * 512 * 512 * 128 + 2 * 8 * 512 * 512 * 128 + 2 * 8 * 512 * 128 * 128
 
-MANUAL = True
 EB = 16
 NCS = 8
-REP = 1
 LAG_M1 = 2
 LAG_M2 = 4
 LAG_GC = 3
@@ -30,15 +28,13 @@ LAG_QG = 3
 LAG_ST = 5
 LAG_FIN = 6
 LAG_CS = 2
-HOFF = 1
 H_AFTER = {0: 0, 2: 1, 3: 2, 4: 3}
 
 
 def tile_rgcnconv_kernel(tc, H, E, RW, SW, out):
     nc = tc.nc
     with ExitStack() as ctx:
-        if MANUAL:
-            ctx.enter_context(tc.manual_schedule())
+        ctx.enter_context(tc.manual_schedule())
         const = ctx.enter_context(tc.tile_pool(name="const", bufs=1))
         epool = ctx.enter_context(tc.tile_pool(name="epool", bufs=EB))
         grpp = ctx.enter_context(tc.tile_pool(name="grpp", bufs=3))
@@ -58,8 +54,6 @@ def tile_rgcnconv_kernel(tc, H, E, RW, SW, out):
         nc.scalar.activation(out=warm[:], in_=warm[:], func=ACT.Sigmoid)
         ones = const.tile([P, NCS], BF16, name="ones")
         nc.vector.memset(ones[:], 1.0)
-        fours = const.tile([P, NCS], BF16, name="fours")
-        nc.vector.memset(fours[:], 4.0)
         ident32 = const.tile([P, P], F32, name="ident32")
         make_identity(nc, ident32[:])
         identbf = const.tile([P, P], BF16, name="identbf")
@@ -84,7 +78,7 @@ def tile_rgcnconv_kernel(tc, H, E, RW, SW, out):
             e_sb = epool.tile([P, NK * 512], BF16, name="e_sb")
             e_dst = e_sb[:].rearrange("p (k j) -> p k j", k=NK)
             e_src = E[b, :, P * c : P * c + P, :].rearrange("k p j -> p k j")
-            step = 2 if n == 0 else NK
+            step = 2 if n < 2 else NK
             for k in range(0, NK, step):
                 nc.sync.dma_start(out=e_dst[:, k : k + step, :], in_=e_src[:, k : k + step, :])
             e_tiles[n] = e_sb
@@ -128,7 +122,7 @@ def tile_rgcnconv_kernel(tc, H, E, RW, SW, out):
             ht_tiles[b] = ht
 
         def self_term(b):
-            sps = gps.tile([P, NC, P], F32, name="sps", tag="gb")
+            sps = xtps.tile([P, NC, P], F32, name="sps", tag="xt")
             ht = ht_tiles[b]
             for c in range(NC):
                 nc.tensor.matmul(
@@ -166,7 +160,6 @@ def tile_rgcnconv_kernel(tc, H, E, RW, SW, out):
                 cs_new = csps.tile([P, NC, NCS], F32, name="cs")
                 cs_tiles[b] = cs_new
             cs = cs_tiles[b]
-            nc.tensor.matmul(out=cs[:, cj, :], lhsT=identbf[:], rhs=fours[:], start=True, stop=False)
             for c in range(NC):
                 for k in range(NK):
                     col = 512 * k + P * cj
@@ -174,7 +167,7 @@ def tile_rgcnconv_kernel(tc, H, E, RW, SW, out):
                         out=cs[:, cj, :],
                         lhsT=e_tiles[NC * b + c][:, col : col + P],
                         rhs=ones[:],
-                        start=False,
+                        start=(c == 0 and k == 0),
                         stop=(c == NC - 1 and k == NK - 1),
                     )
 
@@ -188,20 +181,19 @@ def tile_rgcnconv_kernel(tc, H, E, RW, SW, out):
             b = g // NC
             etq, ets = et_tiles[g]
             gb = gps.tile([P, NK, P], F32, name="gb", tag="gb")
-            for rep in range(REP):
-                nc.tensor.matmul_mx(
-                    out=gb[:].rearrange("m k i -> m (k i)"),
-                    lhsT=hq[:, P * b : P * b + P].bitcast(FP8X4),
-                    lhsT_scale=hs[:, P * b : P * b + P],
-                    rhs=etq[:].bitcast(FP8X4),
-                    rhs_scale=ets[:],
-                    start=True,
-                    stop=True,
-                )
+            nc.tensor.matmul_mx(
+                out=gb[:].rearrange("m k i -> m (k i)"),
+                lhsT=hq[:, P * b : P * b + P].bitcast(FP8X4),
+                lhsT_scale=hs[:, P * b : P * b + P],
+                rhs=etq[:].bitcast(FP8X4),
+                rhs_scale=ets[:],
+                start=True,
+                stop=True,
+            )
             gb_tiles[g] = gb
 
         def on_scalar(g):
-            return g % 8 == 1 or g >= UNITS - NC and g % 2 == 1
+            return g % 8 == 1 or g >= UNITS - 3
 
         def copy_g(g):
             g2 = g2p.tile([P, P, NK], BF16, name="g2", align_bytes=64)
@@ -250,7 +242,8 @@ def tile_rgcnconv_kernel(tc, H, E, RW, SW, out):
 
         def degree_inverse(b):
             d = dpool.tile([P, NC], F32, name="d")
-            nc.vector.reciprocal(out=d[:], in_=cs_tiles[b][:, :, 0])
+            nc.vector.tensor_scalar_add(out=d[:], in0=cs_tiles[b][:, :, 0], scalar1=4.0)
+            nc.vector.reciprocal(out=d[:], in_=d[:])
             d_tiles[b] = d
 
         def finish(b, c0, c1):
@@ -272,11 +265,10 @@ def tile_rgcnconv_kernel(tc, H, E, RW, SW, out):
                 colsums((n - LAG_CS) // NC, (n - LAG_CS) % NC)
             if n + EB < UNITS:
                 load_e(n + EB)
-            m = n - HOFF
-            if 0 <= m < 2 * NB and m % 2 == 0:
-                transpose_h(m // 2)
-            if 0 <= m - 1 < 2 * NB and (m - 1) % 2 == 0:
-                self_term((m - 1) // 2)
+            if n % 2 == 1 and n // 2 < NB:
+                transpose_h(n // 2)
+            if n % 2 == 0 and 0 < n <= 2 * NB:
+                self_term(n // 2 - 1)
             if live(n - LAG_M1):
                 stage1(n - LAG_M1)
             if live(n - LAG_M2):
@@ -285,12 +277,12 @@ def tile_rgcnconv_kernel(tc, H, E, RW, SW, out):
                 copy_g(n - LAG_GC)
             if live(n - LAG_QE):
                 quantise_e(n - LAG_QE)
-            if live(n - LAG_QG):
-                quantise_g(n - LAG_QG)
             if live(n - LAG_ST):
                 if (n - LAG_ST) % NC == 0:
                     degree_inverse((n - LAG_ST) // NC)
                 combine(n - LAG_ST)
+            if live(n - LAG_QG):
+                quantise_g(n - LAG_QG)
             if n == 0:
                 quantise_h(0)
             if n == 1:

@@ -20,6 +20,7 @@ FLOPS = 2 * 8 * 4 * 512 * 512 * 128 + 2 * 8 * 512 * 512 * 128 + 2 * 8 * 512 * 12
 
 EB = 16
 NCS = 8
+NCW = 20
 LAG_M1 = 2
 LAG_M2 = 4
 LAG_GC = 3
@@ -52,7 +53,7 @@ def tile_rgcnconv_kernel(tc, H, E, RW, SW, out):
         warm = const.tile([P, 1], F32, name="warm")
         nc.vector.memset(warm[:], 0.0)
         nc.scalar.activation(out=warm[:], in_=warm[:], func=ACT.Sigmoid)
-        ones = const.tile([P, NCS], BF16, name="ones")
+        ones = const.tile([P, NCW], BF16, name="ones")
         nc.vector.memset(ones[:], 1.0)
         ident32 = const.tile([P, P], F32, name="ident32")
         make_identity(nc, ident32[:])
@@ -157,16 +158,17 @@ def tile_rgcnconv_kernel(tc, H, E, RW, SW, out):
 
         def colsums(b, cj):
             if cj == 0:
-                cs_new = csps.tile([P, NC, NCS], F32, name="cs")
+                cs_new = csps.tile([P, NC, NCW], F32, name="cs")
                 cs_tiles[b] = cs_new
             cs = cs_tiles[b]
             for c in range(NC):
                 for k in range(NK):
                     col = 512 * k + P * cj
+                    width = NCW if c == 0 and k == 0 else NCS
                     nc.tensor.matmul(
-                        out=cs[:, cj, :],
+                        out=cs[:, cj, :width],
                         lhsT=e_tiles[NC * b + c][:, col : col + P],
-                        rhs=ones[:],
+                        rhs=ones[:, :width],
                         start=(c == 0 and k == 0),
                         stop=(c == NC - 1 and k == NK - 1),
                     )

from contextlib import ExitStack

import concourse.mybir as mybir
from concourse.masks import make_identity

F32 = mybir.dt.float32
BF16 = mybir.dt.bfloat16
U32 = mybir.dt.uint32
U8 = mybir.dt.uint8
FP8X4 = mybir.dt.float8_e4m3fn_x4
ALU = mybir.AluOpType
ACT = mybir.ActivationFunctionType

P = 128
NB = 8
NK = 4
NC = 4
UNITS = NB * NC
FLOPS = 2 * 8 * 4 * 512 * 512 * 128 + 2 * 8 * 512 * 512 * 128 + 2 * 8 * 512 * 128 * 128

EB = 16
NCS = 8
NCW = 20
LAG_M1 = 2
LAG_M2 = 4
LAG_GC = 3
LAG_QE = 1
LAG_QG = 3
LAG_ST = 5
LAG_FIN = 6
LAG_CS = 2
H_AFTER = {0: 0, 2: 1, 3: 2, 4: 3}


def tile_rgcnconv_kernel(tc, H, E, RW, SW, out):
    nc = tc.nc
    with ExitStack() as ctx:
        ctx.enter_context(tc.manual_schedule())
        const = ctx.enter_context(tc.tile_pool(name="const", bufs=1))
        epool = ctx.enter_context(tc.tile_pool(name="epool", bufs=EB))
        grpp = ctx.enter_context(tc.tile_pool(name="grpp", bufs=3))
        etp = ctx.enter_context(tc.tile_pool(name="etp", bufs=4))
        g2p = ctx.enter_context(tc.tile_pool(name="g2p", bufs=3))
        hwp = ctx.enter_context(tc.tile_pool(name="hwp", bufs=2))
        htp = ctx.enter_context(tc.tile_pool(name="htp", bufs=3))
        dpool = ctx.enter_context(tc.tile_pool(name="dpool", bufs=3))
        tpool = ctx.enter_context(tc.tile_pool(name="tpool", bufs=3))
        xtps = ctx.enter_context(tc.psum_pool(name="xtps", bufs=3))
        gps = ctx.enter_context(tc.psum_pool(name="gps", bufs=2))
        relps = ctx.enter_context(tc.psum_pool(name="relps", bufs=2))
        csps = ctx.enter_context(tc.psum_pool(name="csps", bufs=1))

        warm = const.tile([P, 1], F32, name="warm")
        nc.vector.memset(warm[:], 0.0)
        nc.scalar.activation(out=warm[:], in_=warm[:], func=ACT.Sigmoid)
        ones = const.tile([P, NCW], BF16, name="ones")
        nc.vector.memset(ones[:], 1.0)
        ident32 = const.tile([P, P], F32, name="ident32")
        make_identity(nc, ident32[:])
        identbf = const.tile([P, P], BF16, name="identbf")
        make_identity(nc, identbf[:])

        sw_sb = const.tile([P, P], BF16, name="sw_sb")
        nc.scalar.dma_start(out=sw_sb[:], in_=SW)
        rw_sb = const.tile([P, 4 * P], BF16, name="rw_sb", align_bytes=64)
        nc.scalar.dma_start(out=rw_sb[:], in_=RW.rearrange("m f k -> m (f k)"))

        h_sb = const.tile([P, NB * 512], BF16, name="h_sb")
        h_dst = h_sb[:].rearrange("q (g x) -> q g x", x=256)
        h_src = H.rearrange("b (u q e) m -> (b u) q (e m)", u=2, q=P, e=2).rearrange("g q x -> q g x")

        def load_h(j):
            nc.sync.dma_start(out=h_dst[:, 4 * j : 4 * j + 4, :], in_=h_src[:, 4 * j : 4 * j + 4, :])

        e_tiles = {}

        def load_e(n):
            b, c = divmod(n, NC)
            e_sb = epool.tile([P, NK * 512], BF16, name="e_sb")
            e_dst = e_sb[:].rearrange("p (k j) -> p k j", k=NK)
            e_src = E[b, :, P * c : P * c + P, :].rearrange("k p j -> p k j")
            step = 2 if n < 2 else NK
            for k in range(0, NK, step):
                nc.sync.dma_start(out=e_dst[:, k : k + step, :], in_=e_src[:, k : k + step, :])
            e_tiles[n] = e_sb

        for n in range(EB):
            load_e(n)
            if n in H_AFTER:
                load_h(H_AFTER[n])

        wq = const.tile([P, P], U32, name="wq", align_bytes=64)
        ws = const.tile([P, P], U8, name="ws", align_bytes=64)

        hq = const.tile([P, NB * P], U32, name="hq", align_bytes=64)
        hs = const.tile([P, NB * P], U8, name="hs", align_bytes=64)
        self_sb = const.tile([P, NB, 512], F32, name="self_sb")

        def quantise_h(j):
            hgrp = hwp.tile([P, 1024], BF16, name="hgrp", align_bytes=64)
            nc.vector.tensor_copy(
                out=hgrp[:].rearrange("q (b m t) -> q b m t", b=2, m=P, t=4),
                in_=h_sb[:, 1024 * j : 1024 * j + 1024].rearrange("q (b t m) -> q b m t", b=2, t=4, m=P),
            )
            nc.vector.quantize_mx(
                out=hq[:, 256 * j : 256 * j + 256].bitcast(FP8X4),
                scales=hs[:, 256 * j : 256 * j + 256],
                in_=hgrp[:],
            )

        ht_tiles = {}

        def transpose_h(b):
            hps = xtps.tile([P, 4, P], BF16, name="hps", tag="xt")
            for t in range(4):
                col = 512 * b + P * t
                nc.tensor.transpose(hps[:, t, :], h_sb[:, col : col + P], identbf[:])
            ht = htp.tile([P, 512], BF16, name="ht")
            nc.scalar.copy(
                out=ht[:].rearrange("m (u q e) -> m u q e", u=2, q=P, e=2),
                in_=hps[:].rearrange("m (u e) q -> m u q e", u=2, e=2),
            )
            ht_tiles[b] = ht

        def self_term(b):
            sps = xtps.tile([P, NC, P], F32, name="sps", tag="xt")
            ht = ht_tiles[b]
            for c in range(NC):
                nc.tensor.matmul(
                    out=sps[:, c, :], lhsT=ht[:, P * c : P * c + P], rhs=sw_sb[:], start=True, stop=True
                )
            nc.scalar.copy(out=self_sb[:, b, :], in_=sps[:].rearrange("p c f -> p (c f)"))

        grp_tiles = {}
        et_tiles = {}
        gb_tiles = {}
        g2_tiles = {}
        gq_tiles = {}
        rel_tiles = {}
        cs_tiles = {}
        d_tiles = {}
        t_tiles = {}

        def transposes(n):
            e32 = e_tiles[n][:].bitcast(F32)
            grp = grpp.tile([P, 2048], BF16, name="grp", align_bytes=64)
            grp32 = grp[:].bitcast(F32)
            for h in range(2):
                xt = xtps.tile([P, 4, P], F32, name="xt", tag="xt")
                for s in range(4):
                    col = 512 * h + P * s
                    nc.tensor.transpose(xt[:, s, :], e32[:, col : col + P], ident32[:])
                nc.scalar.copy(
                    out=grp32[:, 512 * h : 512 * h + 512].rearrange("q (k p u) -> q k p u", k=2, p=P, u=2),
                    in_=xt[:].rearrange("q (k u) p -> q k p u", k=2, u=2),
                )
            grp_tiles[n] = grp

        def colsums(b, cj):
            if cj == 0:
                cs_new = csps.tile([P, NC, NCW], F32, name="cs")
                cs_tiles[b] = cs_new
            cs = cs_tiles[b]
            for c in range(NC):
                for k in range(NK):
                    col = 512 * k + P * cj
                    width = NCW if c == 0 and k == 0 else NCS
                    nc.tensor.matmul(
                        out=cs[:, cj, :width],
                        lhsT=e_tiles[NC * b + c][:, col : col + P],
                        rhs=ones[:, :width],
                        start=(c == 0 and k == 0),
                        stop=(c == NC - 1 and k == NK - 1),
                    )

        def quantise_e(n):
            etq = etp.tile([P, 512], U32, name="etq", align_bytes=64)
            ets = etp.tile([P, 512], U8, name="ets", align_bytes=64)
            nc.vector.quantize_mx(out=etq[:].bitcast(FP8X4), scales=ets[:], in_=grp_tiles[n][:])
            et_tiles[n] = (etq, ets)

        def stage1(g):
            b = g // NC
            etq, ets = et_tiles[g]
            gb = gps.tile([P, NK, P], F32, name="gb", tag="gb")
            nc.tensor.matmul_mx(
                out=gb[:].rearrange("m k i -> m (k i)"),
                lhsT=hq[:, P * b : P * b + P].bitcast(FP8X4),
                lhsT_scale=hs[:, P * b : P * b + P],
                rhs=etq[:].bitcast(FP8X4),
                rhs_scale=ets[:],
                start=True,
                stop=True,
            )
            gb_tiles[g] = gb

        def on_scalar(g):
            return g % 8 == 1 or g >= UNITS - 3

        def copy_g(g):
            g2 = g2p.tile([P, P, NK], BF16, name="g2", align_bytes=64)
            g_in = gb_tiles[g][:].rearrange("m k i -> m i k")
            if on_scalar(g):
                nc.scalar.copy(out=g2[:], in_=g_in)
            else:
                nc.vector.tensor_copy(out=g2[:], in_=g_in)
            g2_tiles[g] = g2

        def quantise_g(g):
            gq = g2p.tile([P, P], U32, name="gq", align_bytes=64)
            gs = g2p.tile([P, P], U8, name="gs", align_bytes=64)
            nc.vector.quantize_mx(
                out=gq[:].bitcast(FP8X4), scales=gs[:], in_=g2_tiles[g][:].rearrange("m i k -> m (i k)")
            )
            gq_tiles[g] = (gq, gs)

        def stage2(g):
            rel = relps.tile([P, P], F32, name="rel")
            gq, gs = gq_tiles[g]
            nc.tensor.matmul_mx(
                out=rel[:],
                lhsT=gq[:].bitcast(FP8X4),
                lhsT_scale=gs[:],
                rhs=wq[:].bitcast(FP8X4),
                rhs_scale=ws[:],
                start=True,
                stop=True,
            )
            rel_tiles[g] = rel

        def combine(g):
            b, c = divmod(g, NC)
            if c == 0:
                t_new = tpool.tile([P, NC, P], F32, name="t")
                t_tiles[b] = t_new
            nc.vector.scalar_tensor_tensor(
                out=t_tiles[b][:, c, :],
                in0=rel_tiles[g][:],
                scalar=d_tiles[b][:, c : c + 1],
                in1=self_sb[:, b, P * c : P * c + P],
                op0=ALU.mult,
                op1=ALU.add,
            )

        def degree_inverse(b):
            d = dpool.tile([P, NC], F32, name="d")
            nc.vector.tensor_scalar_add(out=d[:], in0=cs_tiles[b][:, :, 0], scalar1=4.0)
            nc.vector.reciprocal(out=d[:], in_=d[:])
            d_tiles[b] = d

        def finish(b, c0, c1):
            t = t_tiles[b]
            nc.scalar.activation(out=t[:, c0:c1, :], in_=t[:, c0:c1, :], func=ACT.Sigmoid)
            nc.sync.dma_start(
                out=out[b, P * c0 : P * c1, :].rearrange("(c p) f -> p c f", p=P), in_=t[:, c0:c1, :]
            )

        def live(g):
            return 0 <= g < UNITS

        for n in range(UNITS + LAG_FIN + 1):
            if live(n - LAG_GC) and on_scalar(n - LAG_GC):
                copy_g(n - LAG_GC)
            if n < UNITS:
                transposes(n)
            if live(n - LAG_CS):
                colsums((n - LAG_CS) // NC, (n - LAG_CS) % NC)
            if n + EB < UNITS:
                load_e(n + EB)
            if n % 2 == 1 and n // 2 < NB:
                transpose_h(n // 2)
            if n % 2 == 0 and 0 < n <= 2 * NB:
                self_term(n // 2 - 1)
            if live(n - LAG_M1):
                stage1(n - LAG_M1)
            if live(n - LAG_M2):
                stage2(n - LAG_M2)
            if live(n - LAG_GC) and not on_scalar(n - LAG_GC):
                copy_g(n - LAG_GC)
            if live(n - LAG_QE):
                quantise_e(n - LAG_QE)
            if live(n - LAG_ST):
                if (n - LAG_ST) % NC == 0:
                    degree_inverse((n - LAG_ST) // NC)
                combine(n - LAG_ST)
            if live(n - LAG_QG):
                quantise_g(n - LAG_QG)
            if n == 0:
                quantise_h(0)
            if n == 1:
                nc.vector.quantize_mx(out=wq[:].bitcast(FP8X4), scales=ws[:], in_=rw_sb[:])
            if 2 <= n < 5:
                quantise_h(n - 1)
            gf = n - LAG_FIN
            if live(gf):
                if gf < UNITS - NC:
                    if gf % NC == NC - 1:
                        finish(gf // NC, 0, NC)
                else:
                    finish(NB - 1, gf % NC, gf % NC + 1)
